import numpy as np
import ml_dtypes


def mxq(x, axis, fmt="e4m3"):
    dtype, down = {"e4m3": (ml_dtypes.float8_e4m3fn, 7), "e5m2": (ml_dtypes.float8_e5m2, 14)}[fmt]
    v = np.moveaxis(np.asarray(x, np.float32).astype(ml_dtypes.bfloat16).astype(np.float64), axis, -1)
    blocks = v.reshape(v.shape[:-1] + (-1, 32))
    amax = np.abs(blocks).max(-1, keepdims=True)
    byte = np.maximum(np.where(amax > 0, np.frexp(amax)[1] - 1 + 127, 0) - down, 1)
    scale = np.exp2(byte - 127.0)
    codes = (blocks / scale).astype(np.float32).astype(dtype).astype(np.float64)
    return np.moveaxis((codes * scale).reshape(v.shape), -1, axis)


WIDE = False


def mx_kscale(k):
    if not WIDE:
        return np.ones(k)
    levels = np.array([10, -10, 5, -5, 0])
    a = np.random.permutation(np.resize(levels, k // 512 * 4)).reshape(k // 512, 4)
    idx = np.arange(k)
    return np.exp2(a[idx // 512, idx % 128 // 32])


BF16 = ml_dtypes.bfloat16


def bf(x):
    return np.asarray(x, np.float32).astype(BF16)


def f64(x):
    return np.asarray(x).astype(np.float64)


E2M1 = np.array([0.0, 0.5, 1.0, 1.5, 2.0, 3.0, 4.0, 6.0, -0.0, -0.5, -1.0, -1.5, -2.0, -3.0, -4.0, -6.0])


def pack_weight(w, fmt):
    k, n = w.shape
    w = f64(bf(w)).reshape(k // 32, 32, n)
    amax = np.abs(w).max(1)
    if fmt == "e4m3":
        byte = np.frexp(amax)[1] - 1 + 127 - 7
    else:
        mant, ex = np.frexp(amax / 6.0)
        byte = np.where(mant > 0.5, ex, ex - 1) + 127
    byte = np.clip(np.where(amax > 0, byte, 1), 1, 254)
    scaled = (w * np.exp2(127.0 - byte)[:, None, :]).reshape(k, n).astype(np.float32)
    by_word = np.ascontiguousarray(scaled.reshape(k // 512, 128, 4, n).transpose(0, 1, 3, 2))
    if fmt == "e4m3":
        words = by_word.astype(ml_dtypes.float8_e4m3fn).view(np.uint8)
    else:
        c = by_word.astype(ml_dtypes.float4_e2m1fn).view(np.uint8) & 0xF
        words = c[..., 0::2] | (c[..., 1::2] << 4)
    return np.ascontiguousarray(words), np.ascontiguousarray(byte.astype(np.uint8).reshape(k // 512, 16, n))


def unpack_weight(words, scales, fmt):
    g, p, n, _ = words.shape
    if fmt == "e4m3":
        vals = np.ascontiguousarray(words).view(ml_dtypes.float8_e4m3fn).astype(np.float64)
    else:
        nib = np.empty((g, p, n, 4), np.uint8)
        nib[..., 0::2] = words & 0xF
        nib[..., 1::2] = words >> 4
        vals = E2M1[nib]
    vals = vals * np.repeat(np.exp2(scales.astype(np.float64) - 127.0), 8, axis=1)[..., None]
    return vals.transpose(0, 1, 3, 2).reshape(g * 512, n)


B, T, D, H, HD, Q_STRIDE, WINDOW, QKV = 1, 8192, 512, 8, 64, 64, 128, 3
NW = T // (Q_STRIDE * WINDOW)
SEQ = T // NW
FMT = "e4m3"


def setup_inputs():
    s = mx_kscale(SEQ)
    t = mx_kscale(D)
    g = np.exp(np.random.standard_normal((B, H, NW, SEQ // Q_STRIDE, SEQ)) * 1.3)
    vd = np.random.standard_normal((B, NW, SEQ, D)) * t / s[:, None]
    w = np.random.standard_normal((D, D)) * 5.0 / np.sqrt(D) / t[None, :]
    words, scales = pack_weight(np.ascontiguousarray(w.T), FMT)
    return {"attn": bf(g / g.sum(-1, keepdims=True) * s),
            "v": bf(np.ascontiguousarray(vd.reshape(B, NW, SEQ, H, HD).transpose(0, 3, 1, 2, 4))),
            "proj_w_words": words,
            "proj_w_scales": scales,
            "proj_b": bf(np.random.standard_normal(D) * 0.2)}


def reference(attn, v, proj_w_words, proj_w_scales, proj_b):
    o = mxq(f64(attn), 4, "e4m3") @ mxq(f64(v), 3, "e4m3")
    o = o.transpose(0, 3, 2, 1, 4).reshape(B, -1, H * HD)
    return (mxq(o, 2, "e4m3") @ unpack_weight(proj_w_words, proj_w_scales, FMT)) + f64(proj_b)

@@ -1,0 +1,238 @@
+from contextlib import ExitStack
+
+import concourse.mybir as mybir
+from concourse.masks import make_identity
+
+F32 = mybir.dt.float32
+BF16 = mybir.dt.bfloat16
+I32 = mybir.dt.int32
+U32 = mybir.dt.uint32
+U8 = mybir.dt.uint8
+FP8X4 = mybir.dt.float8_e4m3fn_x4
+
+P = 128
+PACK = 4
+K_PASS = P * PACK
+WORDS_PASS = K_PASS // 2
+
+HEADS = 8
+HEAD_DIM = 64
+QUERIES = 128
+KEYS = 8192
+CHANNELS = HEADS * HEAD_DIM
+
+PAIR = 2
+PAIR_COLS = PAIR * HEAD_DIM
+STEP_PASSES = 4
+STEP_KEYS = STEP_PASSES * K_PASS
+STEPS_PER_PAIR = KEYS // STEP_KEYS
+STEPS = (HEADS // PAIR) * STEPS_PER_PAIR
+BANK_PASSES = 2
+PREFETCH = 8
+
+FLOPS = 2 * HEADS * QUERIES * KEYS * HEAD_DIM + 2 * QUERIES * CHANNELS * CHANNELS
+
+
+def transpose_pass(nc, bank_pass, words, g, identity):
+    for u in range(2):
+        nc.tensor.transpose(
+            bank_pass[:, u, :],
+            words[:, WORDS_PASS * g + u : WORDS_PASS * (g + 1) : 2],
+            identity,
+        )
+
+
+def tile_hieramaskunitattention_pb_k_kernel(
+    tc, attn, v, proj_w_words, proj_w_scales, proj_b, out
+):
+    nc = tc.nc
+    with ExitStack() as stack:
+        const = stack.enter_context(tc.tile_pool(name="const", bufs=1))
+        raw = stack.enter_context(tc.tile_pool(name="raw", bufs=PREFETCH))
+        grouped = stack.enter_context(tc.tile_pool(name="grouped", bufs=3))
+        quantised = stack.enter_context(tc.tile_pool(name="quantised", bufs=3))
+        banks = stack.enter_context(tc.psum_pool(name="banks", bufs=6))
+        sums = stack.enter_context(tc.psum_pool(name="sums", bufs=1))
+        stack.enter_context(tc.manual_schedule())
+
+        v_raw = {}
+        attn_raw = {}
+        v_grouped = {}
+        v_codes = {}
+        v_scales = {}
+        attn_grouped = {}
+        attn_codes = {}
+        attn_scales = {}
+        head_sum = {}
+
+        def load(s):
+            first_head = PAIR * (s // STEPS_PER_PAIR)
+            first_key = STEP_KEYS * (s % STEPS_PER_PAIR)
+            keys = slice(first_key, first_key + STEP_KEYS)
+            for e in range(PAIR):
+                v_raw[s, e] = raw.tile(
+                    [P, STEP_PASSES, PACK, HEAD_DIM], BF16, name="v_raw%d" % e
+                )
+                nc.sync.dma_start(
+                    out=v_raw[s, e][:],
+                    in_=v[0, first_head + e, 0, keys, :].rearrange(
+                        "(g p j) d -> p g j d", p=P, j=PACK
+                    ),
+                )
+            for e in range(PAIR):
+                attn_raw[s, e] = raw.tile([P, STEP_KEYS], BF16, name="attn_raw%d" % e)
+                nc.sync.dma_start(
+                    out=attn_raw[s, e][:], in_=attn[0, first_head + e, 0, :, keys]
+                )
+
+        def regroup_v(s):
+            v_grouped[s] = grouped.tile(
+                [P, STEP_PASSES, PAIR, HEAD_DIM, PACK], BF16, name="v_grouped", align_bytes=64
+            )
+            for e in range(PAIR):
+                nc.vector.tensor_copy(
+                    out=v_grouped[s][:, :, e, :, :].rearrange("p g (c i) j -> p g c j i", i=4),
+                    in_=v_raw[s, e][:].rearrange("p g j (c i) -> p g c j i", i=4),
+                )
+
+        def quantise_v(s):
+            v_codes[s] = quantised.tile(
+                [P, STEP_PASSES * PAIR_COLS], U32, name="v_codes", align_bytes=64
+            )
+            v_scales[s] = quantised.tile(
+                [P, STEP_PASSES * PAIR_COLS], U8, name="v_scales", align_bytes=64
+            )
+            nc.vector.quantize_mx(
+                out=v_codes[s][:].bitcast(FP8X4),
+                scales=v_scales[s][:],
+                in_=v_grouped[s][:].rearrange("p g e d j -> p (g e d j)"),
+            )
+
+        def transpose_attn(s):
+            for e in range(PAIR):
+                attn_grouped[s, e] = grouped.tile(
+                    [P, STEP_PASSES, QUERIES, PACK], BF16, name="attn_grouped%d" % e, align_bytes=64
+                )
+                words = attn_raw[s, e][:].bitcast(F32)
+                for first_pass in range(0, STEP_PASSES, BANK_PASSES):
+                    bank = banks.tile([P, BANK_PASSES, 2, QUERIES], F32, name="bank")
+                    for a in range(BANK_PASSES):
+                        transpose_pass(nc, bank[:, a, :, :], words, first_pass + a, identity[:])
+                    nc.scalar.copy(
+                        out=attn_grouped[s, e][
+                            :, first_pass : first_pass + BANK_PASSES, :, :
+                        ].bitcast(F32),
+                        in_=bank[:].rearrange("p a u q -> p a q u"),
+                    )
+
+        def quantise_attn(s):
+            for e in range(PAIR):
+                attn_codes[s, e] = quantised.tile(
+                    [P, STEP_PASSES * QUERIES], U32, name="attn_codes%d" % e, align_bytes=64
+                )
+                attn_scales[s, e] = quantised.tile(
+                    [P, STEP_PASSES * QUERIES], U8, name="attn_scales%d" % e, align_bytes=64
+                )
+                nc.vector.quantize_mx(
+                    out=attn_codes[s, e][:].bitcast(FP8X4),
+                    scales=attn_scales[s, e][:],
+                    in_=attn_grouped[s, e][:].rearrange("p g q t -> p (g q t)"),
+                )
+
+        def multiply(s):
+            first_head = PAIR * (s // STEPS_PER_PAIR)
+            first_step = s % STEPS_PER_PAIR == 0
+            last_step = s % STEPS_PER_PAIR == STEPS_PER_PAIR - 1
+            for e in range(PAIR):
+                if first_step:
+                    head_sum[e] = sums.tile([P, PAIR_COLS], F32, name="head_sum%d" % e)
+                for g in range(STEP_PASSES):
+                    q_cols = slice(QUERIES * g, QUERIES * (g + 1))
+                    v_cols = slice(PAIR_COLS * g, PAIR_COLS * (g + 1))
+                    nc.tensor.matmul_mx(
+                        out=head_sum[e][:],
+                        lhsT=attn_codes[s, e][:, q_cols].bitcast(FP8X4),
+                        lhsT_scale=attn_scales[s, e][:, q_cols],
+                        rhs=v_codes[s][:, v_cols].bitcast(FP8X4),
+                        rhs_scale=v_scales[s][:, v_cols],
+                        start=first_step and g == 0,
+                        stop=last_step and g == STEP_PASSES - 1,
+                    )
+            if last_step:
+                for e in range(PAIR):
+                    head = first_head + e
+                    nc.scalar.copy(
+                        out=merged[:, HEAD_DIM * head : HEAD_DIM * (head + 1)],
+                        in_=head_sum[e][:, HEAD_DIM * e : HEAD_DIM * (e + 1)],
+                    )
+
+        identity = const.tile([P, P], F32, name="identity")
+        make_identity(nc, identity[:])
+        merged = const.tile([P, CHANNELS], BF16, name="merged")
+
+        bias_rows = const.tile([P, CHANNELS], BF16, name="bias_rows")
+        ones = const.tile([P, P], BF16, name="ones")
+        bias = const.tile([P, CHANNELS], F32, name="bias")
+        nc.vector.memset(bias_rows[:], 0.0)
+        nc.vector.memset(ones[:], 1.0)
+        nc.scalar.dma_start(out=bias_rows[0:1, :], in_=proj_b.rearrange("(o n) -> o n", o=1))
+
+        w_codes = const.tile([P, CHANNELS], U32, name="w_codes", align_bytes=64)
+        w_scales = const.tile([P, CHANNELS], U8, name="w_scales", align_bytes=64)
+        nc.vector.memset(w_scales[:].bitcast(I32), 0)
+
+        for s in range(PREFETCH):
+            load(s)
+        nc.sync.dma_start(
+            out=w_codes[:].bitcast(I32),
+            in_=proj_w_words[0].rearrange("p n t -> p (n t)").bitcast(I32),
+        )
+        for quadrant in range(4):
+            nc.sync.dma_start(
+                out=w_scales[32 * quadrant : 32 * quadrant + 4, :].bitcast(I32),
+                in_=proj_w_scales[0, 4 * quadrant : 4 * quadrant + 4, :].bitcast(I32),
+            )
+
+        bias_bank = banks.tile([P, CHANNELS], F32, name="bank")
+        nc.tensor.matmul(out=bias_bank[:], lhsT=ones[:], rhs=bias_rows[:], start=True, stop=True)
+        nc.vector.tensor_copy(out=bias[:], in_=bias_bank[:])
+
+        for s in range(STEPS + 1):
+            if s < STEPS:
+                regroup_v(s)
+                transpose_attn(s)
+            if s + PREFETCH < STEPS:
+                load(s + PREFETCH)
+            if s >= 1:
+                quantise_attn(s - 1)
+            if s < STEPS:
+                quantise_v(s)
+            if s >= 1:
+                multiply(s - 1)
+
+        merged_bank = banks.tile([P, 2, QUERIES], F32, name="bank")
+        transpose_pass(nc, merged_bank[:], merged[:].bitcast(F32), 0, identity[:])
+        merged_grouped = const.tile([P, QUERIES, PACK], BF16, name="merged_grouped", align_bytes=64)
+        nc.vector.tensor_copy(
+            out=merged_grouped[:].bitcast(F32), in_=merged_bank[:].rearrange("p u q -> p q u")
+        )
+        merged_codes = const.tile([P, QUERIES], U32, name="merged_codes", align_bytes=64)
+        merged_scales = const.tile([P, QUERIES], U8, name="merged_scales", align_bytes=64)
+        nc.vector.quantize_mx(
+            out=merged_codes[:].bitcast(FP8X4),
+            scales=merged_scales[:],
+            in_=merged_grouped[:].rearrange("p q t -> p (q t)"),
+        )
+        out_bank = banks.tile([P, CHANNELS], F32, name="bank")
+        nc.tensor.matmul_mx(
+            out=out_bank[:],
+            lhsT=merged_codes[:].bitcast(FP8X4),
+            lhsT_scale=merged_scales[:],
+            rhs=w_codes[:].bitcast(FP8X4),
+            rhs_scale=w_scales[:],
+            start=True,
+            stop=True,
+        )
+        result = const.tile([P, CHANNELS], F32, name="result")
+        nc.vector.tensor_add(out=result[:], in0=out_bank[:], in1=bias[:])
+        nc.sync.dma_start(out=out[0], in_=result[:])

@@ -33,6 +33,12 @@ PREFETCH = 8
 FLOPS = 2 * HEADS * QUERIES * KEYS * HEAD_DIM + 2 * QUERIES * CHANNELS * CHANNELS
 
 
+def transpose_pass_halves(nc, bank_pass, words, g, identity):
+    for u in range(2):
+        first_word = WORDS_PASS * g + P * u
+        nc.tensor.transpose(bank_pass[:, u, :], words[:, first_word : first_word + P], identity)
+
+
 def transpose_pass(nc, bank_pass, words, g, identity):
     for u in range(2):
         nc.tensor.transpose(
@@ -74,9 +80,9 @@ def tile_hieramaskunitattention_pb_k_kernel(
                     [P, STEP_PASSES, PACK, HEAD_DIM], BF16, name="v_raw%d" % e
                 )
                 nc.sync.dma_start(
-                    out=v_raw[s, e][:],
+                    out=v_raw[s, e][:].rearrange("p g (u i) d -> p (g u) (i d)", u=2),
                     in_=v[0, first_head + e, 0, keys, :].rearrange(
-                        "(g p j) d -> p g j d", p=P, j=PACK
+                        "(m p i) d -> p m (i d)", p=P, i=2
                     ),
                 )
             for e in range(PAIR):
@@ -117,7 +123,7 @@ def tile_hieramaskunitattention_pb_k_kernel(
                 for first_pass in range(0, STEP_PASSES, BANK_PASSES):
                     bank = banks.tile([P, BANK_PASSES, 2, QUERIES], F32, name="bank")
                     for a in range(BANK_PASSES):
-                        transpose_pass(nc, bank[:, a, :, :], words, first_pass + a, identity[:])
+                        transpose_pass_halves(nc, bank[:, a, :, :], words, first_pass + a, identity[:])
                     nc.scalar.copy(
                         out=attn_grouped[s, e][
                             :, first_pass : first_pass + BANK_PASSES, :, :

@@ -33,12 +33,6 @@ PREFETCH = 8
 FLOPS = 2 * HEADS * QUERIES * KEYS * HEAD_DIM + 2 * QUERIES * CHANNELS * CHANNELS
 
 
-def transpose_pass_halves(nc, bank_pass, words, g, identity):
-    for u in range(2):
-        first_word = WORDS_PASS * g + P * u
-        nc.tensor.transpose(bank_pass[:, u, :], words[:, first_word : first_word + P], identity)
-
-
 def transpose_pass(nc, bank_pass, words, g, identity):
     for u in range(2):
         nc.tensor.transpose(
@@ -80,9 +74,9 @@ def tile_hieramaskunitattention_pb_k_kernel(
                     [P, STEP_PASSES, PACK, HEAD_DIM], BF16, name="v_raw%d" % e
                 )
                 nc.sync.dma_start(
-                    out=v_raw[s, e][:].rearrange("p g (u i) d -> p (g u) (i d)", u=2),
+                    out=v_raw[s, e][:],
                     in_=v[0, first_head + e, 0, keys, :].rearrange(
-                        "(m p i) d -> p m (i d)", p=P, i=2
+                        "(g p j) d -> p g j d", p=P, j=PACK
                     ),
                 )
             for e in range(PAIR):
@@ -123,7 +117,7 @@ def tile_hieramaskunitattention_pb_k_kernel(
                 for first_pass in range(0, STEP_PASSES, BANK_PASSES):
                     bank = banks.tile([P, BANK_PASSES, 2, QUERIES], F32, name="bank")
                     for a in range(BANK_PASSES):
-                        transpose_pass_halves(nc, bank[:, a, :, :], words, first_pass + a, identity[:])
+                        transpose_pass(nc, bank[:, a, :, :], words, first_pass + a, identity[:])
                     nc.scalar.copy(
                         out=attn_grouped[s, e][
                             :, first_pass : first_pass + BANK_PASSES, :, :
@@ -187,17 +181,18 @@ def tile_hieramaskunitattention_pb_k_kernel(
         w_scales = const.tile([P, CHANNELS], U8, name="w_scales", align_bytes=64)
         nc.vector.memset(w_scales[:].bitcast(I32), 0)
 
-        for s in range(PREFETCH):
-            load(s)
-        nc.sync.dma_start(
-            out=w_codes[:].bitcast(I32),
-            in_=proj_w_words[0].rearrange("p n t -> p (n t)").bitcast(I32),
+        nc.gpsimd.dma_start(
+            out=w_codes[:].bitcast(F32),
+            in_=proj_w_words[0].rearrange("p n t -> p (n t)").bitcast(F32),
         )
         for quadrant in range(4):
-            nc.sync.dma_start(
-                out=w_scales[32 * quadrant : 32 * quadrant + 4, :].bitcast(I32),
-                in_=proj_w_scales[0, 4 * quadrant : 4 * quadrant + 4, :].bitcast(I32),
+            nc.gpsimd.dma_start(
+                out=w_scales[32 * quadrant : 32 * quadrant + 4, :].bitcast(F32),
+                in_=proj_w_scales[0, 4 * quadrant : 4 * quadrant + 4, :].bitcast(F32),
             )
+
+        for s in range(PREFETCH):
+            load(s)
 
         bias_bank = banks.tile([P, CHANNELS], F32, name="bank")
         nc.tensor.matmul(out=bias_bank[:], lhsT=ones[:], rhs=bias_rows[:], start=True, stop=True)

@@ -23,10 +23,11 @@ CHANNELS = HEADS * HEAD_DIM
 
 PAIR = 2
 PAIR_COLS = PAIR * HEAD_DIM
+PAIRS = HEADS // PAIR
+HEAD_PASSES = KEYS // K_PASS
 STEP_PASSES = 4
-STEP_KEYS = STEP_PASSES * K_PASS
-STEPS_PER_PAIR = KEYS // STEP_KEYS
-STEPS = (HEADS // PAIR) * STEPS_PER_PAIR
+LAST_PAIR_STEPS = (4, 4, 4, 2, 1, 1)
+BIAS_STEP = 6
 BANK_PASSES = 2
 PREFETCH = 8
 
@@ -65,13 +66,27 @@ def tile_hieramaskunitattention_pb_k_kernel(
         attn_scales = {}
         head_sum = {}
 
+        pair_of = []
+        first_pass = []
+        passes = []
+        for pair in range(PAIRS):
+            sizes = (STEP_PASSES,) * (HEAD_PASSES // STEP_PASSES)
+            if pair == PAIRS - 1:
+                sizes = LAST_PAIR_STEPS
+            start = 0
+            for size in sizes:
+                pair_of.append(pair)
+                first_pass.append(start)
+                passes.append(size)
+                start += size
+        steps = len(passes)
+
         def load(s):
-            first_head = PAIR * (s // STEPS_PER_PAIR)
-            first_key = STEP_KEYS * (s % STEPS_PER_PAIR)
-            keys = slice(first_key, first_key + STEP_KEYS)
+            first_head = PAIR * pair_of[s]
+            keys = slice(K_PASS * first_pass[s], K_PASS * (first_pass[s] + passes[s]))
             for e in range(PAIR):
                 v_raw[s, e] = raw.tile(
-                    [P, STEP_PASSES, PACK, HEAD_DIM], BF16, name="v_raw%d" % e
+                    [P, passes[s], PACK, HEAD_DIM], BF16, name="v_raw%d" % e
                 )
                 nc.sync.dma_start(
                     out=v_raw[s, e][:],
@@ -80,14 +95,14 @@ def tile_hieramaskunitattention_pb_k_kernel(
                     ),
                 )
             for e in range(PAIR):
-                attn_raw[s, e] = raw.tile([P, STEP_KEYS], BF16, name="attn_raw%d" % e)
+                attn_raw[s, e] = raw.tile([P, K_PASS * passes[s]], BF16, name="attn_raw%d" % e)
                 nc.sync.dma_start(
                     out=attn_raw[s, e][:], in_=attn[0, first_head + e, 0, :, keys]
                 )
 
         def regroup_v(s):
             v_grouped[s] = grouped.tile(
-                [P, STEP_PASSES, PAIR, HEAD_DIM, PACK], BF16, name="v_grouped", align_bytes=64
+                [P, passes[s], PAIR, HEAD_DIM, PACK], BF16, name="v_grouped", align_bytes=64
             )
             for e in range(PAIR):
                 nc.vector.tensor_copy(
@@ -97,10 +112,10 @@ def tile_hieramaskunitattention_pb_k_kernel(
 
         def quantise_v(s):
             v_codes[s] = quantised.tile(
-                [P, STEP_PASSES * PAIR_COLS], U32, name="v_codes", align_bytes=64
+                [P, passes[s] * PAIR_COLS], U32, name="v_codes", align_bytes=64
             )
             v_scales[s] = quantised.tile(
-                [P, STEP_PASSES * PAIR_COLS], U8, name="v_scales", align_bytes=64
+                [P, passes[s] * PAIR_COLS], U8, name="v_scales", align_bytes=64
             )
             nc.vector.quantize_mx(
                 out=v_codes[s][:].bitcast(FP8X4),
@@ -111,27 +126,26 @@ def tile_hieramaskunitattention_pb_k_kernel(
         def transpose_attn(s):
             for e in range(PAIR):
                 attn_grouped[s, e] = grouped.tile(
-                    [P, STEP_PASSES, QUERIES, PACK], BF16, name="attn_grouped%d" % e, align_bytes=64
+                    [P, passes[s], QUERIES, PACK], BF16, name="attn_grouped%d" % e, align_bytes=64
                 )
                 words = attn_raw[s, e][:].bitcast(F32)
-                for first_pass in range(0, STEP_PASSES, BANK_PASSES):
-                    bank = banks.tile([P, BANK_PASSES, 2, QUERIES], F32, name="bank")
-                    for a in range(BANK_PASSES):
-                        transpose_pass(nc, bank[:, a, :, :], words, first_pass + a, identity[:])
+                for g in range(0, passes[s], BANK_PASSES):
+                    count = min(BANK_PASSES, passes[s] - g)
+                    bank = banks.tile([P, count, 2, QUERIES], F32, name="bank")
+                    for a in range(count):
+                        transpose_pass(nc, bank[:, a, :, :], words, g + a, identity[:])
                     nc.scalar.copy(
-                        out=attn_grouped[s, e][
-                            :, first_pass : first_pass + BANK_PASSES, :, :
-                        ].bitcast(F32),
+                        out=attn_grouped[s, e][:, g : g + count, :, :].bitcast(F32),
                         in_=bank[:].rearrange("p a u q -> p a q u"),
                     )
 
         def quantise_attn(s):
             for e in range(PAIR):
                 attn_codes[s, e] = quantised.tile(
-                    [P, STEP_PASSES * QUERIES], U32, name="attn_codes%d" % e, align_bytes=64
+                    [P, passes[s] * QUERIES], U32, name="attn_codes%d" % e, align_bytes=64
                 )
                 attn_scales[s, e] = quantised.tile(
-                    [P, STEP_PASSES * QUERIES], U8, name="attn_scales%d" % e, align_bytes=64
+                    [P, passes[s] * QUERIES], U8, name="attn_scales%d" % e, align_bytes=64
                 )
                 nc.vector.quantize_mx(
                     out=attn_codes[s, e][:].bitcast(FP8X4),
@@ -140,13 +154,13 @@ def tile_hieramaskunitattention_pb_k_kernel(
                 )
 
         def multiply(s):
-            first_head = PAIR * (s // STEPS_PER_PAIR)
-            first_step = s % STEPS_PER_PAIR == 0
-            last_step = s % STEPS_PER_PAIR == STEPS_PER_PAIR - 1
+            first_head = PAIR * pair_of[s]
+            first_step = first_pass[s] == 0
+            last_step = first_pass[s] + passes[s] == HEAD_PASSES
             for e in range(PAIR):
                 if first_step:
                     head_sum[e] = sums.tile([P, PAIR_COLS], F32, name="head_sum%d" % e)
-                for g in range(STEP_PASSES):
+                for g in range(passes[s]):
                     q_cols = slice(QUERIES * g, QUERIES * (g + 1))
                     v_cols = slice(PAIR_COLS * g, PAIR_COLS * (g + 1))
                     nc.tensor.matmul_mx(
@@ -156,7 +170,7 @@ def tile_hieramaskunitattention_pb_k_kernel(
                         rhs=v_codes[s][:, v_cols].bitcast(FP8X4),
                         rhs_scale=v_scales[s][:, v_cols],
                         start=first_step and g == 0,
-                        stop=last_step and g == STEP_PASSES - 1,
+                        stop=last_step and g == passes[s] - 1,
                     )
             if last_step:
                 for e in range(PAIR):
@@ -194,19 +208,21 @@ def tile_hieramaskunitattention_pb_k_kernel(
         for s in range(PREFETCH):
             load(s)
 
-        bias_bank = banks.tile([P, CHANNELS], F32, name="bank")
-        nc.tensor.matmul(out=bias_bank[:], lhsT=ones[:], rhs=bias_rows[:], start=True, stop=True)
-        nc.vector.tensor_copy(out=bias[:], in_=bias_bank[:])
-
-        for s in range(STEPS + 1):
-            if s < STEPS:
+        for s in range(steps + 1):
+            if s == BIAS_STEP:
+                bias_bank = banks.tile([P, CHANNELS], F32, name="bank")
+                nc.tensor.matmul(
+                    out=bias_bank[:], lhsT=ones[:], rhs=bias_rows[:], start=True, stop=True
+                )
+                nc.vector.tensor_copy(out=bias[:], in_=bias_bank[:])
+            if s < steps:
                 regroup_v(s)
                 transpose_attn(s)
-            if s + PREFETCH < STEPS:
+            if s + PREFETCH < steps:
                 load(s + PREFETCH)
             if s >= 1:
                 quantise_attn(s - 1)
-            if s < STEPS:
+            if s < steps:
                 quantise_v(s)
             if s >= 1:
                 multiply(s - 1)

@@ -86,7 +86,7 @@ def tile_hieramaskunitattention_pb_k_kernel(
             keys = slice(K_PASS * first_pass[s], K_PASS * (first_pass[s] + passes[s]))
             for e in range(PAIR):
                 v_raw[s, e] = raw.tile(
-                    [P, passes[s], PACK, HEAD_DIM], BF16, name="v_raw%d" % e
+                    [P, passes[s], PACK, HEAD_DIM], BF16, name="v_raw%d" % e, align_bytes=512
                 )
                 nc.sync.dma_start(
                     out=v_raw[s, e][:],
@@ -95,7 +95,9 @@ def tile_hieramaskunitattention_pb_k_kernel(
                     ),
                 )
             for e in range(PAIR):
-                attn_raw[s, e] = raw.tile([P, K_PASS * passes[s]], BF16, name="attn_raw%d" % e)
+                attn_raw[s, e] = raw.tile(
+                    [P, K_PASS * passes[s]], BF16, name="attn_raw%d" % e, align_bytes=512
+                )
                 nc.sync.dma_start(
                     out=attn_raw[s, e][:], in_=attn[0, first_head + e, 0, :, keys]
                 )

@@ -28,6 +28,7 @@ HEAD_PASSES = KEYS // K_PASS
 STEP_PASSES = 4
 LAST_PAIR_STEPS = (4, 4, 4, 2, 1, 1)
 BIAS_STEP = 6
+OUT_COLS = 256
 BANK_PASSES = 2
 PREFETCH = 8
 
@@ -100,6 +101,17 @@ def tile_hieramaskunitattention_pb_k_kernel(
                 )
                 nc.sync.dma_start(
                     out=attn_raw[s, e][:], in_=attn[0, first_head + e, 0, :, keys]
+                )
+
+        def load_w():
+            nc.sync.dma_start(
+                out=w_codes[:].bitcast(I32),
+                in_=proj_w_words[0].rearrange("p n t -> p (n t)").bitcast(I32),
+            )
+            for quadrant in range(4):
+                nc.sync.dma_start(
+                    out=w_scales[32 * quadrant : 32 * quadrant + 4, :].bitcast(I32),
+                    in_=proj_w_scales[0, 4 * quadrant : 4 * quadrant + 4, :].bitcast(I32),
                 )
 
         def regroup_v(s):
@@ -197,16 +209,6 @@ def tile_hieramaskunitattention_pb_k_kernel(
         w_scales = const.tile([P, CHANNELS], U8, name="w_scales", align_bytes=64)
         nc.vector.memset(w_scales[:].bitcast(I32), 0)
 
-        nc.gpsimd.dma_start(
-            out=w_codes[:].bitcast(F32),
-            in_=proj_w_words[0].rearrange("p n t -> p (n t)").bitcast(F32),
-        )
-        for quadrant in range(4):
-            nc.gpsimd.dma_start(
-                out=w_scales[32 * quadrant : 32 * quadrant + 4, :].bitcast(F32),
-                in_=proj_w_scales[0, 4 * quadrant : 4 * quadrant + 4, :].bitcast(F32),
-            )
-
         for s in range(PREFETCH):
             load(s)
 
@@ -216,23 +218,26 @@ def tile_hieramaskunitattention_pb_k_kernel(
                 nc.tensor.matmul(
                     out=bias_bank[:], lhsT=ones[:], rhs=bias_rows[:], start=True, stop=True
                 )
-                nc.vector.tensor_copy(out=bias[:], in_=bias_bank[:])
             if s < steps:
                 regroup_v(s)
                 transpose_attn(s)
             if s + PREFETCH < steps:
                 load(s + PREFETCH)
+            if s + PREFETCH == steps:
+                load_w()
             if s >= 1:
                 quantise_attn(s - 1)
             if s < steps:
                 quantise_v(s)
+            if s == BIAS_STEP:
+                nc.vector.tensor_copy(out=bias[:], in_=bias_bank[:])
             if s >= 1:
                 multiply(s - 1)
 
         merged_bank = banks.tile([P, 2, QUERIES], F32, name="bank")
         transpose_pass(nc, merged_bank[:], merged[:].bitcast(F32), 0, identity[:])
         merged_grouped = const.tile([P, QUERIES, PACK], BF16, name="merged_grouped", align_bytes=64)
-        nc.vector.tensor_copy(
+        nc.scalar.copy(
             out=merged_grouped[:].bitcast(F32), in_=merged_bank[:].rearrange("p u q -> p q u")
         )
         merged_codes = const.tile([P, QUERIES], U32, name="merged_codes", align_bytes=64)
@@ -242,16 +247,18 @@ def tile_hieramaskunitattention_pb_k_kernel(
             scales=merged_scales[:],
             in_=merged_grouped[:].rearrange("p q t -> p (q t)"),
         )
-        out_bank = banks.tile([P, CHANNELS], F32, name="bank")
-        nc.tensor.matmul_mx(
-            out=out_bank[:],
-            lhsT=merged_codes[:].bitcast(FP8X4),
-            lhsT_scale=merged_scales[:],
-            rhs=w_codes[:].bitcast(FP8X4),
-            rhs_scale=w_scales[:],
-            start=True,
-            stop=True,
-        )
-        result = const.tile([P, CHANNELS], F32, name="result")
-        nc.vector.tensor_add(out=result[:], in0=out_bank[:], in1=bias[:])
-        nc.sync.dma_start(out=out[0], in_=result[:])
+        for first in range(0, CHANNELS, OUT_COLS):
+            cols = slice(first, first + OUT_COLS)
+            out_bank = banks.tile([P, OUT_COLS], F32, name="bank")
+            nc.tensor.matmul_mx(
+                out=out_bank[:],
+                lhsT=merged_codes[:].bitcast(FP8X4),
+                lhsT_scale=merged_scales[:],
+                rhs=w_codes[:, cols].bitcast(FP8X4),
+                rhs_scale=w_scales[:, cols],
+                start=True,
+                stop=True,
+            )
+            result = const.tile([P, OUT_COLS], F32, name="result%d" % first)
+            nc.vector.tensor_add(out=result[:], in0=out_bank[:], in1=bias[:, cols])
+            nc.sync.dma_start(out=out[0, :, cols], in_=result[:])

@@ -25,12 +25,13 @@ PAIR = 2
 PAIR_COLS = PAIR * HEAD_DIM
 PAIRS = HEADS // PAIR
 HEAD_PASSES = KEYS // K_PASS
+LOAD_PASSES = ((4, 4, 8), (8, 8), (8, 4, 4), (4, 4, 4, 2, 2))
 STEP_PASSES = 4
-LAST_PAIR_STEPS = (4, 4, 4, 2, 1, 1)
+LAST_RUN_STEPS = 3
 BIAS_STEP = 6
 OUT_COLS = 256
 BANK_PASSES = 2
-PREFETCH = 8
+PREFETCH = 5
 
 FLOPS = 2 * HEADS * QUERIES * KEYS * HEAD_DIM + 2 * QUERIES * CHANNELS * CHANNELS
 
@@ -67,40 +68,45 @@ def tile_hieramaskunitattention_pb_k_kernel(
         attn_scales = {}
         head_sum = {}
 
+        loads = []
         pair_of = []
         first_pass = []
         passes = []
+        load_of = []
+        load_pass = []
         for pair in range(PAIRS):
-            sizes = (STEP_PASSES,) * (HEAD_PASSES // STEP_PASSES)
-            if pair == PAIRS - 1:
-                sizes = LAST_PAIR_STEPS
             start = 0
-            for size in sizes:
-                pair_of.append(pair)
-                first_pass.append(start)
-                passes.append(size)
-                start += size
+            for count in LOAD_PASSES[pair]:
+                for offset in range(0, count, STEP_PASSES):
+                    pair_of.append(pair)
+                    first_pass.append(start + offset)
+                    passes.append(min(STEP_PASSES, count - offset))
+                    load_of.append(len(loads))
+                    load_pass.append(offset)
+                loads.append((pair, start, count))
+                start += count
         steps = len(passes)
 
-        def load(s):
-            first_head = PAIR * pair_of[s]
-            keys = slice(K_PASS * first_pass[s], K_PASS * (first_pass[s] + passes[s]))
+        def load(n):
+            pair, start, count = loads[n]
+            first_head = PAIR * pair
+            keys = slice(K_PASS * start, K_PASS * (start + count))
             for e in range(PAIR):
-                v_raw[s, e] = raw.tile(
-                    [P, passes[s], PACK, HEAD_DIM], BF16, name="v_raw%d" % e, align_bytes=512
+                v_raw[n, e] = raw.tile(
+                    [P, count, PACK, HEAD_DIM], BF16, name="v_raw%d" % e, align_bytes=512
                 )
                 nc.sync.dma_start(
-                    out=v_raw[s, e][:],
+                    out=v_raw[n, e][:],
                     in_=v[0, first_head + e, 0, keys, :].rearrange(
                         "(g p j) d -> p g j d", p=P, j=PACK
                     ),
                 )
             for e in range(PAIR):
-                attn_raw[s, e] = raw.tile(
-                    [P, K_PASS * passes[s]], BF16, name="attn_raw%d" % e, align_bytes=512
+                attn_raw[n, e] = raw.tile(
+                    [P, K_PASS * count], BF16, name="attn_raw%d" % e, align_bytes=512
                 )
                 nc.sync.dma_start(
-                    out=attn_raw[s, e][:], in_=attn[0, first_head + e, 0, :, keys]
+                    out=attn_raw[n, e][:], in_=attn[0, first_head + e, 0, :, keys]
                 )
 
         def load_w():
@@ -118,10 +124,11 @@ def tile_hieramaskunitattention_pb_k_kernel(
             v_grouped[s] = grouped.tile(
                 [P, passes[s], PAIR, HEAD_DIM, PACK], BF16, name="v_grouped", align_bytes=64
             )
+            of_load = slice(load_pass[s], load_pass[s] + passes[s])
             for e in range(PAIR):
                 nc.vector.tensor_copy(
                     out=v_grouped[s][:, :, e, :, :].rearrange("p g (c i) j -> p g c j i", i=4),
-                    in_=v_raw[s, e][:].rearrange("p g j (c i) -> p g c j i", i=4),
+                    in_=v_raw[load_of[s], e][:, of_load].rearrange("p g j (c i) -> p g c j i", i=4),
                 )
 
         def quantise_v(s):
@@ -142,12 +149,14 @@ def tile_hieramaskunitattention_pb_k_kernel(
                 attn_grouped[s, e] = grouped.tile(
                     [P, passes[s], QUERIES, PACK], BF16, name="attn_grouped%d" % e, align_bytes=64
                 )
-                words = attn_raw[s, e][:].bitcast(F32)
+                words = attn_raw[load_of[s], e][:].bitcast(F32)
                 for g in range(0, passes[s], BANK_PASSES):
                     count = min(BANK_PASSES, passes[s] - g)
                     bank = banks.tile([P, count, 2, QUERIES], F32, name="bank")
                     for a in range(count):
-                        transpose_pass(nc, bank[:, a, :, :], words, g + a, identity[:])
+                        transpose_pass(
+                            nc, bank[:, a, :, :], words, load_pass[s] + g + a, identity[:]
+                        )
                     nc.scalar.copy(
                         out=attn_grouped[s, e][:, g : g + count, :, :].bitcast(F32),
                         in_=bank[:].rearrange("p a u q -> p a q u"),
@@ -209,8 +218,8 @@ def tile_hieramaskunitattention_pb_k_kernel(
         w_scales = const.tile([P, CHANNELS], U8, name="w_scales", align_bytes=64)
         nc.vector.memset(w_scales[:].bitcast(I32), 0)
 
-        for s in range(PREFETCH):
-            load(s)
+        for n in range(PREFETCH):
+            load(n)
 
         for s in range(steps + 1):
             if s == BIAS_STEP:
@@ -221,18 +230,22 @@ def tile_hieramaskunitattention_pb_k_kernel(
             if s < steps:
                 regroup_v(s)
                 transpose_attn(s)
-            if s + PREFETCH < steps:
-                load(s + PREFETCH)
-            if s + PREFETCH == steps:
-                load_w()
+            if s < steps and load_of[s] != load_of[min(s + 1, steps - 1)]:
+                n = load_of[s] + PREFETCH
+                if n < len(loads):
+                    load(n)
+                if n == len(loads):
+                    load_w()
             if s >= 1:
                 quantise_attn(s - 1)
             if s < steps:
                 quantise_v(s)
             if s == BIAS_STEP:
                 nc.vector.tensor_copy(out=bias[:], in_=bias_bank[:])
-            if s >= 1:
+            if 1 <= s <= steps - LAST_RUN_STEPS:
                 multiply(s - 1)
+        for s in range(steps - LAST_RUN_STEPS, steps):
+            multiply(s)
 
         merged_bank = banks.tile([P, 2, QUERIES], F32, name="bank")
         transpose_pass(nc, merged_bank[:], merged[:].bitcast(F32), 0, identity[:])

@@ -126,10 +126,14 @@ def tile_hieramaskunitattention_pb_k_kernel(
             )
             of_load = slice(load_pass[s], load_pass[s] + passes[s])
             for e in range(PAIR):
-                nc.vector.tensor_copy(
-                    out=v_grouped[s][:, :, e, :, :].rearrange("p g (c i) j -> p g c j i", i=4),
-                    in_=v_raw[load_of[s], e][:, of_load].rearrange("p g j (c i) -> p g c j i", i=4),
-                )
+                own = passes[s]
+                if e == PAIR - 1 and passes[s] == STEP_PASSES:
+                    own = passes[s] // 2
+                src = v_raw[load_of[s], e][:, of_load].rearrange("p g j (c i) -> p g c j i", i=4)
+                dst = v_grouped[s][:, :, e, :, :].rearrange("p g (c i) j -> p g c j i", i=4)
+                nc.vector.tensor_copy(out=dst[:, :own], in_=src[:, :own])
+                if own < passes[s]:
+                    nc.scalar.copy(out=dst[:, own:], in_=src[:, own:])
 
         def quantise_v(s):
             v_codes[s] = quantised.tile(

from contextlib import ExitStack

import concourse.mybir as mybir
from concourse.masks import make_identity

F32 = mybir.dt.float32
BF16 = mybir.dt.bfloat16
I32 = mybir.dt.int32
U32 = mybir.dt.uint32
U8 = mybir.dt.uint8
FP8X4 = mybir.dt.float8_e4m3fn_x4

P = 128
PACK = 4
K_PASS = P * PACK
WORDS_PASS = K_PASS // 2

HEADS = 8
HEAD_DIM = 64
QUERIES = 128
KEYS = 8192
CHANNELS = HEADS * HEAD_DIM

PAIR = 2
PAIR_COLS = PAIR * HEAD_DIM
PAIRS = HEADS // PAIR
HEAD_PASSES = KEYS // K_PASS
LOAD_PASSES = ((4, 4, 8), (8, 8), (8, 4, 4), (4, 4, 4, 2, 2))
STEP_PASSES = 4
LAST_RUN_STEPS = 3
BIAS_STEP = 6
OUT_COLS = 256
BANK_PASSES = 2
PREFETCH = 5

FLOPS = 2 * HEADS * QUERIES * KEYS * HEAD_DIM + 2 * QUERIES * CHANNELS * CHANNELS


def transpose_pass(nc, bank_pass, words, g, identity):
    for u in range(2):
        nc.tensor.transpose(
            bank_pass[:, u, :],
            words[:, WORDS_PASS * g + u : WORDS_PASS * (g + 1) : 2],
            identity,
        )


def tile_hieramaskunitattention_pb_k_kernel(
    tc, attn, v, proj_w_words, proj_w_scales, proj_b, out
):
    nc = tc.nc
    with ExitStack() as stack:
        const = stack.enter_context(tc.tile_pool(name="const", bufs=1))
        raw = stack.enter_context(tc.tile_pool(name="raw", bufs=PREFETCH))
        grouped = stack.enter_context(tc.tile_pool(name="grouped", bufs=3))
        quantised = stack.enter_context(tc.tile_pool(name="quantised", bufs=3))
        banks = stack.enter_context(tc.psum_pool(name="banks", bufs=6))
        sums = stack.enter_context(tc.psum_pool(name="sums", bufs=1))
        stack.enter_context(tc.manual_schedule())

        v_raw = {}
        attn_raw = {}
        v_grouped = {}
        v_codes = {}
        v_scales = {}
        attn_grouped = {}
        attn_codes = {}
        attn_scales = {}
        head_sum = {}

        loads = []
        pair_of = []
        first_pass = []
        passes = []
        load_of = []
        load_pass = []
        for pair in range(PAIRS):
            start = 0
            for count in LOAD_PASSES[pair]:
                for offset in range(0, count, STEP_PASSES):
                    pair_of.append(pair)
                    first_pass.append(start + offset)
                    passes.append(min(STEP_PASSES, count - offset))
                    load_of.append(len(loads))
                    load_pass.append(offset)
                loads.append((pair, start, count))
                start += count
        steps = len(passes)

        def load(n):
            pair, start, count = loads[n]
            first_head = PAIR * pair
            keys = slice(K_PASS * start, K_PASS * (start + count))
            for e in range(PAIR):
                v_raw[n, e] = raw.tile(
                    [P, count, PACK, HEAD_DIM], BF16, name="v_raw%d" % e, align_bytes=512
                )
                nc.sync.dma_start(
                    out=v_raw[n, e][:],
                    in_=v[0, first_head + e, 0, keys, :].rearrange(
                        "(g p j) d -> p g j d", p=P, j=PACK
                    ),
                )
            for e in range(PAIR):
                attn_raw[n, e] = raw.tile(
                    [P, K_PASS * count], BF16, name="attn_raw%d" % e, align_bytes=512
                )
                nc.sync.dma_start(
                    out=attn_raw[n, e][:], in_=attn[0, first_head + e, 0, :, keys]
                )

        def load_w():
            nc.sync.dma_start(
                out=w_codes[:].bitcast(I32),
                in_=proj_w_words[0].rearrange("p n t -> p (n t)").bitcast(I32),
            )
            for quadrant in range(4):
                nc.sync.dma_start(
                    out=w_scales[32 * quadrant : 32 * quadrant + 4, :].bitcast(I32),
                    in_=proj_w_scales[0, 4 * quadrant : 4 * quadrant + 4, :].bitcast(I32),
                )

        def regroup_v(s):
            v_grouped[s] = grouped.tile(
                [P, passes[s], PAIR, HEAD_DIM, PACK], BF16, name="v_grouped", align_bytes=64
            )
            of_load = slice(load_pass[s], load_pass[s] + passes[s])
            for e in range(PAIR):
                own = passes[s]
                if e == PAIR - 1 and passes[s] == STEP_PASSES:
                    own = passes[s] // 2
                src = v_raw[load_of[s], e][:, of_load].rearrange("p g j (c i) -> p g c j i", i=4)
                dst = v_grouped[s][:, :, e, :, :].rearrange("p g (c i) j -> p g c j i", i=4)
                nc.vector.tensor_copy(out=dst[:, :own], in_=src[:, :own])
                if own < passes[s]:
                    nc.scalar.copy(out=dst[:, own:], in_=src[:, own:])

        def quantise_v(s):
            v_codes[s] = quantised.tile(
                [P, passes[s] * PAIR_COLS], U32, name="v_codes", align_bytes=64
            )
            v_scales[s] = quantised.tile(
                [P, passes[s] * PAIR_COLS], U8, name="v_scales", align_bytes=64
            )
            nc.vector.quantize_mx(
                out=v_codes[s][:].bitcast(FP8X4),
                scales=v_scales[s][:],
                in_=v_grouped[s][:].rearrange("p g e d j -> p (g e d j)"),
            )

        def transpose_attn(s):
            for e in range(PAIR):
                attn_grouped[s, e] = grouped.tile(
                    [P, passes[s], QUERIES, PACK], BF16, name="attn_grouped%d" % e, align_bytes=64
                )
                words = attn_raw[load_of[s], e][:].bitcast(F32)
                for g in range(0, passes[s], BANK_PASSES):
                    count = min(BANK_PASSES, passes[s] - g)
                    bank = banks.tile([P, count, 2, QUERIES], F32, name="bank")
                    for a in range(count):
                        transpose_pass(
                            nc, bank[:, a, :, :], words, load_pass[s] + g + a, identity[:]
                        )
                    nc.scalar.copy(
                        out=attn_grouped[s, e][:, g : g + count, :, :].bitcast(F32),
                        in_=bank[:].rearrange("p a u q -> p a q u"),
                    )

        def quantise_attn(s):
            for e in range(PAIR):
                attn_codes[s, e] = quantised.tile(
                    [P, passes[s] * QUERIES], U32, name="attn_codes%d" % e, align_bytes=64
                )
                attn_scales[s, e] = quantised.tile(
                    [P, passes[s] * QUERIES], U8, name="attn_scales%d" % e, align_bytes=64
                )
                nc.vector.quantize_mx(
                    out=attn_codes[s, e][:].bitcast(FP8X4),
                    scales=attn_scales[s, e][:],
                    in_=attn_grouped[s, e][:].rearrange("p g q t -> p (g q t)"),
                )

        def multiply(s):
            first_head = PAIR * pair_of[s]
            first_step = first_pass[s] == 0
            last_step = first_pass[s] + passes[s] == HEAD_PASSES
            for e in range(PAIR):
                if first_step:
                    head_sum[e] = sums.tile([P, PAIR_COLS], F32, name="head_sum%d" % e)
                for g in range(passes[s]):
                    q_cols = slice(QUERIES * g, QUERIES * (g + 1))
                    v_cols = slice(PAIR_COLS * g, PAIR_COLS * (g + 1))
                    nc.tensor.matmul_mx(
                        out=head_sum[e][:],
                        lhsT=attn_codes[s, e][:, q_cols].bitcast(FP8X4),
                        lhsT_scale=attn_scales[s, e][:, q_cols],
                        rhs=v_codes[s][:, v_cols].bitcast(FP8X4),
                        rhs_scale=v_scales[s][:, v_cols],
                        start=first_step and g == 0,
                        stop=last_step and g == passes[s] - 1,
                    )
            if last_step:
                for e in range(PAIR):
                    head = first_head + e
                    nc.scalar.copy(
                        out=merged[:, HEAD_DIM * head : HEAD_DIM * (head + 1)],
                        in_=head_sum[e][:, HEAD_DIM * e : HEAD_DIM * (e + 1)],
                    )

        identity = const.tile([P, P], F32, name="identity")
        make_identity(nc, identity[:])
        merged = const.tile([P, CHANNELS], BF16, name="merged")

        bias_rows = const.tile([P, CHANNELS], BF16, name="bias_rows")
        ones = const.tile([P, P], BF16, name="ones")
        bias = const.tile([P, CHANNELS], F32, name="bias")
        nc.vector.memset(bias_rows[:], 0.0)
        nc.vector.memset(ones[:], 1.0)
        nc.scalar.dma_start(out=bias_rows[0:1, :], in_=proj_b.rearrange("(o n) -> o n", o=1))

        w_codes = const.tile([P, CHANNELS], U32, name="w_codes", align_bytes=64)
        w_scales = const.tile([P, CHANNELS], U8, name="w_scales", align_bytes=64)
        nc.vector.memset(w_scales[:].bitcast(I32), 0)

        for n in range(PREFETCH):
            load(n)

        for s in range(steps + 1):
            if s == BIAS_STEP:
                bias_bank = banks.tile([P, CHANNELS], F32, name="bank")
                nc.tensor.matmul(
                    out=bias_bank[:], lhsT=ones[:], rhs=bias_rows[:], start=True, stop=True
                )
            if s < steps:
                regroup_v(s)
                transpose_attn(s)
            if s < steps and load_of[s] != load_of[min(s + 1, steps - 1)]:
                n = load_of[s] + PREFETCH
                if n < len(loads):
                    load(n)
                if n == len(loads):
                    load_w()
            if s >= 1:
                quantise_attn(s - 1)
            if s < steps:
                quantise_v(s)
            if s == BIAS_STEP:
                nc.vector.tensor_copy(out=bias[:], in_=bias_bank[:])
            if 1 <= s <= steps - LAST_RUN_STEPS:
                multiply(s - 1)
        for s in range(steps - LAST_RUN_STEPS, steps):
            multiply(s)

        merged_bank = banks.tile([P, 2, QUERIES], F32, name="bank")
        transpose_pass(nc, merged_bank[:], merged[:].bitcast(F32), 0, identity[:])
        merged_grouped = const.tile([P, QUERIES, PACK], BF16, name="merged_grouped", align_bytes=64)
        nc.scalar.copy(
            out=merged_grouped[:].bitcast(F32), in_=merged_bank[:].rearrange("p u q -> p q u")
        )
        merged_codes = const.tile([P, QUERIES], U32, name="merged_codes", align_bytes=64)
        merged_scales = const.tile([P, QUERIES], U8, name="merged_scales", align_bytes=64)
        nc.vector.quantize_mx(
            out=merged_codes[:].bitcast(FP8X4),
            scales=merged_scales[:],
            in_=merged_grouped[:].rearrange("p q t -> p (q t)"),
        )
        for first in range(0, CHANNELS, OUT_COLS):
            cols = slice(first, first + OUT_COLS)
            out_bank = banks.tile([P, OUT_COLS], F32, name="bank")
            nc.tensor.matmul_mx(
                out=out_bank[:],
                lhsT=merged_codes[:].bitcast(FP8X4),
                lhsT_scale=merged_scales[:],
                rhs=w_codes[:, cols].bitcast(FP8X4),
                rhs_scale=w_scales[:, cols],
                start=True,
                stop=True,
            )
            result = const.tile([P, OUT_COLS], F32, name="result%d" % first)
            nc.vector.tensor_add(out=result[:], in0=out_bank[:], in1=bias[:, cols])
            nc.sync.dma_start(out=out[0, :, cols], in_=result[:])
